import numpy as np
import ml_dtypes


def mxq(x, axis, fmt="e4m3"):
    dtype, down = {"e4m3": (ml_dtypes.float8_e4m3fn, 7), "e5m2": (ml_dtypes.float8_e5m2, 14)}[fmt]
    v = np.moveaxis(np.asarray(x, np.float32).astype(ml_dtypes.bfloat16).astype(np.float64), axis, -1)
    blocks = v.reshape(v.shape[:-1] + (-1, 32))
    amax = np.abs(blocks).max(-1, keepdims=True)
    byte = np.maximum(np.where(amax > 0, np.frexp(amax)[1] - 1 + 127, 0) - down, 1)
    scale = np.exp2(byte - 127.0)
    codes = (blocks / scale).astype(np.float32).astype(dtype).astype(np.float64)
    return np.moveaxis((codes * scale).reshape(v.shape), -1, axis)


WIDE = False


def mx_kscale(k):
    if not WIDE:
        return np.ones(k)
    levels = np.array([10, -10, 5, -5, 0])
    if k % 512:
        return np.exp2(np.random.permutation(np.resize(levels, k // 32))).repeat(32)
    a = np.empty((k // 512, 16))
    for p in range(k // 512):
        a[p, :8] = np.random.permutation(np.resize(levels, 8))
        for g in range(8):
            far = levels[np.abs(levels - a[p, g]) >= 10]
            a[p, g + 8] = far[np.random.randint(len(far))]
    return np.exp2(a.ravel()).repeat(32)


BF16 = ml_dtypes.bfloat16


def bf(x):
    return np.asarray(x, np.float32).astype(BF16)


def f64(x):
    return np.asarray(x).astype(np.float64)


B, S, D, E = 4, 1024, 512, 2
K = E * D


def setup_inputs():
    s = mx_kscale(K)
    return {"att": bf(np.random.standard_normal((E, B, S, D)) * 0.3 * s.reshape(E, 1, 1, D)),
            "scene_reps": bf(np.random.standard_normal((B, S, D))),
            "Wo": bf(np.random.standard_normal((D, K)) * 2.0 / np.sqrt(K) / s[None, :]),
            "bo": bf(np.random.standard_normal(D) * 0.1),
            "gamma": bf(1.0 + np.random.standard_normal(D) * 0.1),
            "beta": bf(np.random.standard_normal(D) * 0.1)}


def reference(att, scene_reps, Wo, bo, gamma, beta):
    cat = np.moveaxis(f64(att), 0, 2).reshape(B, S, K)
    fused = (mxq(cat, 2, "e4m3") @ mxq(f64(Wo), 1, "e4m3").T) + f64(bo)
    y = f64(scene_reps) + fused
    mu = y.mean(-1, keepdims=True)
    var = y.var(-1, keepdims=True)
    return (y - mu) / np.sqrt(var + 1e-5) * f64(gamma) + f64(beta)

@@ -1,0 +1,286 @@
+from contextlib import ExitStack
+
+import concourse.mybir as mybir
+from concourse.masks import make_identity
+
+F32 = mybir.dt.float32
+BF16 = mybir.dt.bfloat16
+U32 = mybir.dt.uint32
+U8 = mybir.dt.uint8
+FP8X4 = mybir.dt.float8_e4m3fn_x4
+ALU = mybir.AluOpType
+ACT = mybir.ActivationFunctionType
+
+P = 128
+D = 512
+E = 2
+TOKENS = 4096
+TILES = TOKENS // P
+PAIRS = TILES // 2
+LOAD_TILES = 4
+LOADS = TILES // LOAD_TILES
+WORDS = D // 2
+EPS = 1e-5
+FLOPS = 2 * TOKENS * E * D * D
+
+
+def tile_heterogeneousgraphtransformer_pb_t_kernel(tc, att, scene_reps, Wo, bo, gamma, beta, out):
+    nc = tc.nc
+    att_v = att.rearrange("e b s d -> e (b s) d").rearrange("e (p j) d -> p e j d", j=TILES)
+    scene_v = scene_reps.rearrange("b s d -> (b s) d").rearrange("(p j) d -> p j d", j=TILES)
+    out_v = out.rearrange("b s d -> (b s) d").rearrange("(p j) d -> p j d", j=TILES)
+    wo_v = Wo.rearrange("(t p) k -> p t k", p=P)
+
+    with ExitStack() as ctx:
+        const = ctx.enter_context(tc.tile_pool(name="const", bufs=1))
+        loads = ctx.enter_context(tc.tile_pool(name="loads", bufs=LOADS))
+        grp_pool = ctx.enter_context(tc.tile_pool(name="grp", bufs=3))
+        code_pool = ctx.enter_context(tc.tile_pool(name="code", bufs=3))
+        sb_pool = ctx.enter_context(tc.tile_pool(name="sb", bufs=3))
+        o_pool = ctx.enter_context(tc.tile_pool(name="o", bufs=10))
+        small = ctx.enter_context(tc.tile_pool(name="small", bufs=4))
+        ps_const = ctx.enter_context(tc.psum_pool(name="psc", bufs=1))
+        ps_xt = ctx.enter_context(tc.psum_pool(name="psx", bufs=2))
+        ps_f = ctx.enter_context(tc.psum_pool(name="psf", bufs=4))
+        ctx.enter_context(tc.manual_schedule())
+
+        vecs = const.tile([P, 3 * D], BF16)
+        nc.vector.memset(vecs[:], 0.0)
+        ones = const.tile([P, P], BF16)
+        nc.vector.memset(ones[:], 1.0)
+        eps_t = const.tile([P, 1], F32)
+        nc.vector.memset(eps_t[:], EPS)
+        ident = const.tile([P, P], F32)
+        make_identity(nc, ident[:])
+        warm = const.tile([P, 1], F32)
+        nc.scalar.activation(out=warm[:], in_=eps_t[:], func=ACT.Abs_reciprocal_sqrt)
+        squares_out = const.tile([P, D], F32)
+
+        wo_sb = const.tile([P, 4 * E * D], BF16)
+        for h in range(2):
+            nc.sync.dma_start(
+                out=wo_sb[:, h * 2 * E * D:(h + 1) * 2 * E * D].rearrange("p (t k) -> p t k", t=2),
+                in_=wo_v[:, 2 * h:2 * h + 2, :],
+            )
+        att_t = []
+        scene_t = []
+        for c in range(LOADS):
+            a = loads.tile([P, E * LOAD_TILES * D], BF16, name="att%d" % c, tag="att")
+            s = loads.tile([P, LOAD_TILES * D], BF16, name="scene%d" % c, tag="scene")
+            att_t.append(a)
+            scene_t.append(s)
+            a_v = a[:].rearrange("p (e j d) -> p e j d", e=E, j=LOAD_TILES)
+            s_v = s[:].rearrange("p (j d) -> p j d", j=LOAD_TILES)
+            if c == 0:
+                nc.sync.dma_start(out=a_v[:, :, 0:2, :], in_=att_v[:, :, 0:2, :])
+                for i, v in enumerate((bo, gamma, beta)):
+                    nc.sync.dma_start(out=vecs[0:1, i * D:(i + 1) * D], in_=v.rearrange("(o d) -> o d", o=1))
+                nc.sync.dma_start(out=s_v, in_=scene_v[:, 0:LOAD_TILES, :])
+                nc.sync.dma_start(out=a_v[:, :, 2:4, :], in_=att_v[:, :, 2:4, :])
+            else:
+                nc.sync.dma_start(out=a_v, in_=att_v[:, :, c * LOAD_TILES:(c + 1) * LOAD_TILES, :])
+                nc.sync.dma_start(out=s_v, in_=scene_v[:, c * LOAD_TILES:(c + 1) * LOAD_TILES, :])
+
+        wo_f = wo_sb[:].bitcast(F32)
+        wgrp = const.tile([P, E * D * 4], BF16, align_bytes=64)
+        wgrp_f = wgrp[:].bitcast(F32)
+        wcodes = const.tile([P, E * D], U32, align_bytes=64)
+        wscl = const.tile([P, E * D], U8, align_bytes=64)
+        for h in range(2):
+            for e in range(E):
+                wt = ps_f.tile([P, D], F32, name="wt%d%d" % (h, e), tag="f")
+                for t in range(2):
+                    for u in range(2):
+                        w0 = ((2 * h + t) * E + e) * WORDS
+                        nc.tensor.transpose(
+                            out=wt[:, (t * 2 + u) * P:(t * 2 + u + 1) * P], in_=wo_f[:, w0 + u:w0 + WORDS:2],
+                            identity=ident[:],
+                        )
+                dst = wgrp_f[:, (e * D + h * 2 * P) * 2:(e * D + (h + 1) * 2 * P) * 2].rearrange(
+                    "p (t r u) -> p t r u", t=2, u=2)
+                src = wt[:].rearrange("p (t u r) -> p t r u", t=2, u=2)
+                if e == 0:
+                    nc.vector.tensor_copy(out=dst, in_=src)
+                else:
+                    nc.scalar.copy(out=dst, in_=src)
+            for e in range(E):
+                c0 = e * D + h * 2 * P
+                nc.vector.quantize_mx(
+                    out=wcodes[:, c0:c0 + 2 * P].bitcast(FP8X4),
+                    scales=wscl[:, c0:c0 + 2 * P],
+                    in_=wgrp[:, 4 * c0:4 * (c0 + 2 * P)],
+                )
+
+        xt_t = {}
+        grp_t = {}
+        code_t = {}
+        scl_t = {}
+        sb_t = {}
+        f_t = {}
+        o_t = {}
+        sums_t = {}
+        negmean_t = {}
+        sumsq_t = {}
+        rstd_t = {}
+
+        def transposes(k):
+            if k >= PAIRS:
+                return
+            a_f = att_t[k // 2][:].bitcast(F32)
+            for i in range(2):
+                j = 2 * (k % 2) + i
+                xt = ps_xt.tile([P, D], F32, name="xt%d_%d" % (k, i), tag="xt")
+                xt_t[(k, i)] = xt
+                for e in range(E):
+                    for u in range(2):
+                        w0 = (e * LOAD_TILES + j) * WORDS
+                        nc.tensor.transpose(
+                            out=xt[:, (e * 2 + u) * P:(e * 2 + u + 1) * P], in_=a_f[:, w0 + u:w0 + WORDS:2],
+                            identity=ident[:],
+                        )
+
+        def regroup(k, i):
+            if k >= PAIRS:
+                return
+            if i == 0:
+                grp_t[k] = grp_pool.tile([P, 2 * E * P * 4], BF16, name="grp%d" % k, tag="grp", align_bytes=64)
+            g_f = grp_t[k][:].bitcast(F32)
+            nc.scalar.copy(
+                out=g_f[:, i * D:(i + 1) * D].rearrange("p (e r u) -> p e r u", e=E, u=2),
+                in_=xt_t[(k, i)][:].rearrange("p (e u r) -> p e r u", e=E, u=2),
+            )
+
+        def quantise(k):
+            if k >= PAIRS:
+                return
+            code_t[k] = code_pool.tile([P, 2 * E * P], U32, name="cd%d" % k, tag="cd", align_bytes=64)
+            scl_t[k] = code_pool.tile([P, 2 * E * P], U8, name="sc%d" % k, tag="sc", align_bytes=64)
+            nc.vector.quantize_mx(out=code_t[k][:].bitcast(FP8X4), scales=scl_t[k][:], in_=grp_t[k][:])
+
+        def matmuls(k):
+            if k >= PAIRS:
+                return
+            for i in range(2):
+                f = ps_f.tile([P, D], F32, name="f%d_%d" % (k, i), tag="f")
+                f_t[(k, i)] = f
+                for e in range(E):
+                    cols = slice((i * E + e) * P, (i * E + e + 1) * P)
+                    nc.tensor.matmul_mx(
+                        out=f[:],
+                        lhsT=code_t[k][:, cols].bitcast(FP8X4),
+                        lhsT_scale=scl_t[k][:, cols],
+                        rhs=wcodes[:, e * D:(e + 1) * D].bitcast(FP8X4),
+                        rhs_scale=wscl[:, e * D:(e + 1) * D],
+                        start=(e == 0),
+                        stop=(e == E - 1),
+                    )
+
+        def add_bias(k, engine):
+            if k >= PAIRS:
+                return
+            sb_t[k] = sb_pool.tile([P, 2 * D], F32, name="sb%d" % k, tag="sb")
+            s0 = 2 * (k % 2) * D
+            for i in range(2):
+                engine.tensor_tensor(
+                    out=sb_t[k][:, i * D:(i + 1) * D],
+                    in0=scene_t[k // 2][:, s0 + i * D:s0 + (i + 1) * D],
+                    in1=bo_b[:],
+                    op=ALU.add,
+                )
+
+        def residual(k, i):
+            if i == 0:
+                sums_t[k] = small.tile([P, 2], F32, name="sums%d" % k, tag="sums")
+            y = sb_t[k][:, i * D:(i + 1) * D]
+            nc.vector.scalar_tensor_tensor(
+                out=y, in0=y, scalar=1.0, in1=f_t[(k, i)][:], op0=ALU.mult, op1=ALU.add,
+                accum_out=sums_t[k][:, i:i + 1],
+            )
+
+        def squares(k, i):
+            if i == 0:
+                negmean_t[k] = small.tile([P, 2], F32, name="negmean%d" % k, tag="negmean")
+                sumsq_t[k] = small.tile([P, 2], F32, name="sumsq%d" % k, tag="sumsq")
+            nc.scalar.activation(
+                out=negmean_t[k][:, i:i + 1], in_=sums_t[k][:, i:i + 1], func=ACT.Copy, scale=-1.0 / D
+            )
+            nc.scalar.activation(
+                out=squares_out[:], in_=sb_t[k][:, i * D:(i + 1) * D], func=ACT.Square,
+                bias=negmean_t[k][:, i:i + 1], scale=1.0, accum_out=sumsq_t[k][:, i:i + 1],
+            )
+
+        def inv_std(k):
+            rstd_t[k] = small.tile([P, 2], F32, name="rstd%d" % k, tag="rstd")
+            nc.scalar.activation(
+                out=rstd_t[k][:], in_=sumsq_t[k][:], func=ACT.Abs_reciprocal_sqrt, bias=eps_t[:], scale=1.0 / D
+            )
+
+        def centre_gain(k, i):
+            if i == 0:
+                o_t[k] = o_pool.tile([P, 2 * D], F32, name="o%d" % k, tag="o")
+            nc.vector.scalar_tensor_tensor(
+                out=o_t[k][:, i * D:(i + 1) * D], in0=sb_t[k][:, i * D:(i + 1) * D],
+                scalar=negmean_t[k][:, i:i + 1], in1=gamma_ps[:], op0=ALU.add, op1=ALU.mult,
+            )
+
+        def scale_shift(k, i):
+            o = o_t[k][:, i * D:(i + 1) * D]
+            nc.vector.scalar_tensor_tensor(
+                out=o, in0=o, scalar=rstd_t[k][:, i:i + 1], in1=beta_ps[:], op0=ALU.mult, op1=ALU.add
+            )
+
+        transposes(0)
+        regroup(0, 0)
+        regroup(0, 1)
+        quantise(0)
+        gamma_ps = ps_const.tile([P, D], F32)
+        beta_ps = ps_const.tile([P, D], F32)
+        bo_ps = ps_xt.tile([P, D], F32, name="bo_ps", tag="xt")
+        nc.tensor.matmul(out=bo_ps[:], lhsT=ones[:], rhs=vecs[:, 0:D], start=True, stop=True)
+        nc.tensor.matmul(out=gamma_ps[:], lhsT=ones[:], rhs=vecs[:, D:2 * D], start=True, stop=True)
+        nc.tensor.matmul(out=beta_ps[:], lhsT=ones[:], rhs=vecs[:, 2 * D:3 * D], start=True, stop=True)
+        bo_b = const.tile([P, D], BF16)
+        nc.vector.tensor_copy(out=bo_b[:], in_=bo_ps[:])
+        add_bias(0, nc.vector)
+        matmuls(0)
+        transposes(1)
+        regroup(1, 0)
+        regroup(1, 1)
+        quantise(1)
+        matmuls(1)
+        transposes(2)
+        add_bias(1, nc.gpsimd)
+        add_bias(2, nc.gpsimd)
+
+        for n in range(PAIRS + 1):
+            m = n - 1
+            if n < PAIRS:
+                residual(n, 0)
+                squares(n, 0)
+                residual(n, 1)
+                squares(n, 1)
+                inv_std(n)
+                if n == 0:
+                    regroup(2, 0)
+                    regroup(2, 1)
+                    transposes(3)
+                regroup(n + 3, 0)
+                regroup(n + 3, 1)
+            if m >= 0:
+                scale_shift(m, 0)
+                if m == PAIRS - 1:
+                    nc.sync.dma_start(out=out_v[:, 2 * m, :], in_=o_t[m][:, 0:D])
+                scale_shift(m, 1)
+                if m == PAIRS - 1:
+                    nc.sync.dma_start(out=out_v[:, 2 * m + 1, :], in_=o_t[m][:, D:2 * D])
+                else:
+                    nc.sync.dma_start(
+                        out=out_v[:, 2 * m:2 * m + 2, :], in_=o_t[m][:].rearrange("p (j d) -> p j d", j=2)
+                    )
+            if n < PAIRS:
+                centre_gain(n, 0)
+                quantise(n + 2)
+                matmuls(n + 2)
+                transposes(n + 4)
+                centre_gain(n, 1)
+                add_bias(n + 3, nc.gpsimd)

@@ -17,8 +17,7 @@ E = 2
 TOKENS = 4096
 TILES = TOKENS // P
 PAIRS = TILES // 2
-LOAD_TILES = 4
-LOADS = TILES // LOAD_TILES
+LOAD_TILES = (2, 2) + (4,) * ((TILES - 4) // 4)
 WORDS = D // 2
 EPS = 1e-5
 FLOPS = 2 * TOKENS * E * D * D
@@ -33,7 +32,7 @@ def tile_heterogeneousgraphtransformer_pb_t_kernel(tc, att, scene_reps, Wo, bo, 
 
     with ExitStack() as ctx:
         const = ctx.enter_context(tc.tile_pool(name="const", bufs=1))
-        loads = ctx.enter_context(tc.tile_pool(name="loads", bufs=LOADS))
+        loads = ctx.enter_context(tc.tile_pool(name="loads", bufs=1))
         grp_pool = ctx.enter_context(tc.tile_pool(name="grp", bufs=3))
         code_pool = ctx.enter_context(tc.tile_pool(name="code", bufs=3))
         sb_pool = ctx.enter_context(tc.tile_pool(name="sb", bufs=3))
@@ -44,72 +43,89 @@ def tile_heterogeneousgraphtransformer_pb_t_kernel(tc, att, scene_reps, Wo, bo, 
         ps_f = ctx.enter_context(tc.psum_pool(name="psf", bufs=4))
         ctx.enter_context(tc.manual_schedule())
 
-        vecs = const.tile([P, 3 * D], BF16)
-        nc.vector.memset(vecs[:], 0.0)
-        ones = const.tile([P, P], BF16)
-        nc.vector.memset(ones[:], 1.0)
-        eps_t = const.tile([P, 1], F32)
-        nc.vector.memset(eps_t[:], EPS)
         ident = const.tile([P, P], F32)
         make_identity(nc, ident[:])
-        warm = const.tile([P, 1], F32)
-        nc.scalar.activation(out=warm[:], in_=eps_t[:], func=ACT.Abs_reciprocal_sqrt)
+        bo_row = const.tile([P, D], BF16)
+        nc.vector.memset(bo_row[:].bitcast(U32), 0)
+        ones = const.tile([P, P], BF16)
+        nc.vector.memset(ones[:], 1.0)
+        gb_rows = const.tile([P, 2 * D], BF16)
+        nc.vector.memset(gb_rows[:].bitcast(U32), 0)
+        eps_t = const.tile([P, 1], F32)
+        nc.vector.memset(eps_t[:], EPS)
         squares_out = const.tile([P, D], F32)
 
-        wo_sb = const.tile([P, 4 * E * D], BF16)
-        for h in range(2):
-            nc.sync.dma_start(
-                out=wo_sb[:, h * 2 * E * D:(h + 1) * 2 * E * D].rearrange("p (t k) -> p t k", t=2),
-                in_=wo_v[:, 2 * h:2 * h + 2, :],
-            )
+        nc.sync.dma_start(out=bo_row[0:1, :], in_=bo.rearrange("(o d) -> o d", o=1))
+        for i, v in enumerate((gamma, beta)):
+            nc.scalar.dma_start(out=gb_rows[0:1, i * D:(i + 1) * D], in_=v.rearrange("(o d) -> o d", o=1))
+        warm = const.tile([P, 1], F32)
+        nc.scalar.activation(out=warm[:], in_=eps_t[:], func=ACT.Abs_reciprocal_sqrt)
+
+        pair_load = []
         att_t = []
         scene_t = []
-        for c in range(LOADS):
-            a = loads.tile([P, E * LOAD_TILES * D], BF16, name="att%d" % c, tag="att")
-            s = loads.tile([P, LOAD_TILES * D], BF16, name="scene%d" % c, tag="scene")
-            att_t.append(a)
-            scene_t.append(s)
-            a_v = a[:].rearrange("p (e j d) -> p e j d", e=E, j=LOAD_TILES)
-            s_v = s[:].rearrange("p (j d) -> p j d", j=LOAD_TILES)
-            if c == 0:
-                nc.sync.dma_start(out=a_v[:, :, 0:2, :], in_=att_v[:, :, 0:2, :])
-                for i, v in enumerate((bo, gamma, beta)):
-                    nc.sync.dma_start(out=vecs[0:1, i * D:(i + 1) * D], in_=v.rearrange("(o d) -> o d", o=1))
-                nc.sync.dma_start(out=s_v, in_=scene_v[:, 0:LOAD_TILES, :])
-                nc.sync.dma_start(out=a_v[:, :, 2:4, :], in_=att_v[:, :, 2:4, :])
-            else:
-                nc.sync.dma_start(out=a_v, in_=att_v[:, :, c * LOAD_TILES:(c + 1) * LOAD_TILES, :])
-                nc.sync.dma_start(out=s_v, in_=scene_v[:, c * LOAD_TILES:(c + 1) * LOAD_TILES, :])
+        for c, n in enumerate(LOAD_TILES):
+            att_t.append(loads.tile([P, E * n * D], BF16, name="att%d" % c))
+            scene_t.append(loads.tile([P, n * D], BF16, name="scene%d" % c))
+            for j in range(0, n, 2):
+                pair_load.append((att_t[c], scene_t[c], n, j))
 
-        wo_f = wo_sb[:].bitcast(F32)
+        def load_att(c):
+            g, n = sum(LOAD_TILES[:c]), LOAD_TILES[c]
+            nc.sync.dma_start(out=att_t[c][:].rearrange("p (e j d) -> p e j d", e=E, j=n), in_=att_v[:, :, g:g + n, :])
+
+        def load_scene(c):
+            g, n = sum(LOAD_TILES[:c]), LOAD_TILES[c]
+            nc.sync.dma_start(out=scene_t[c][:].rearrange("p (j d) -> p j d", j=n), in_=scene_v[:, g:g + n, :])
+
+        wo_sb = []
+        for h in range(2):
+            wo_sb.append(const.tile([P, 2 * E * D], BF16, name="wo%d" % h))
+        load_att(0)
+        load_scene(0)
+        for h in range(2):
+            nc.sync.dma_start(
+                out=wo_sb[h][:].rearrange("p (t k) -> p t k", t=2), in_=wo_v[:, 2 * h:2 * h + 2, :],
+            )
+        load_att(1)
+        load_scene(1)
+        for c in range(2, len(LOAD_TILES)):
+            load_att(c)
+            load_scene(c)
+
         wgrp = const.tile([P, E * D * 4], BF16, align_bytes=64)
         wgrp_f = wgrp[:].bitcast(F32)
         wcodes = const.tile([P, E * D], U32, align_bytes=64)
         wscl = const.tile([P, E * D], U8, align_bytes=64)
-        for h in range(2):
+        wt_t = {}
+
+        def wo_transposes(h):
+            wo_f = wo_sb[h][:].bitcast(F32)
             for e in range(E):
                 wt = ps_f.tile([P, D], F32, name="wt%d%d" % (h, e), tag="f")
+                wt_t[(h, e)] = wt
                 for t in range(2):
                     for u in range(2):
-                        w0 = ((2 * h + t) * E + e) * WORDS
+                        w0 = (t * E + e) * WORDS
                         nc.tensor.transpose(
                             out=wt[:, (t * 2 + u) * P:(t * 2 + u + 1) * P], in_=wo_f[:, w0 + u:w0 + WORDS:2],
                             identity=ident[:],
                         )
-                dst = wgrp_f[:, (e * D + h * 2 * P) * 2:(e * D + (h + 1) * 2 * P) * 2].rearrange(
-                    "p (t r u) -> p t r u", t=2, u=2)
-                src = wt[:].rearrange("p (t u r) -> p t r u", t=2, u=2)
-                if e == 0:
-                    nc.vector.tensor_copy(out=dst, in_=src)
-                else:
-                    nc.scalar.copy(out=dst, in_=src)
-            for e in range(E):
-                c0 = e * D + h * 2 * P
-                nc.vector.quantize_mx(
-                    out=wcodes[:, c0:c0 + 2 * P].bitcast(FP8X4),
-                    scales=wscl[:, c0:c0 + 2 * P],
-                    in_=wgrp[:, 4 * c0:4 * (c0 + 2 * P)],
-                )
+
+        def wo_regroup(h, e, copy):
+            copy(
+                out=wgrp_f[:, (e * D + h * 2 * P) * 2:(e * D + (h + 1) * 2 * P) * 2].rearrange(
+                    "p (t r u) -> p t r u", t=2, u=2),
+                in_=wt_t[(h, e)][:].rearrange("p (t u r) -> p t r u", t=2, u=2),
+            )
+
+        def wo_quantise(h, e):
+            c0 = e * D + h * 2 * P
+            nc.vector.quantize_mx(
+                out=wcodes[:, c0:c0 + 2 * P].bitcast(FP8X4),
+                scales=wscl[:, c0:c0 + 2 * P],
+                in_=wgrp[:, 4 * c0:4 * (c0 + 2 * P)],
+            )
 
         xt_t = {}
         grp_t = {}
@@ -126,14 +142,15 @@ def tile_heterogeneousgraphtransformer_pb_t_kernel(tc, att, scene_reps, Wo, bo, 
         def transposes(k):
             if k >= PAIRS:
                 return
-            a_f = att_t[k // 2][:].bitcast(F32)
+            att_tile, scene_tile, n, j0 = pair_load[k]
+            a_f = att_tile[:].bitcast(F32)
             for i in range(2):
-                j = 2 * (k % 2) + i
+                j = j0 + i
                 xt = ps_xt.tile([P, D], F32, name="xt%d_%d" % (k, i), tag="xt")
                 xt_t[(k, i)] = xt
                 for e in range(E):
                     for u in range(2):
-                        w0 = (e * LOAD_TILES + j) * WORDS
+                        w0 = (e * n + j) * WORDS
                         nc.tensor.transpose(
                             out=xt[:, (e * 2 + u) * P:(e * 2 + u + 1) * P], in_=a_f[:, w0 + u:w0 + WORDS:2],
                             identity=ident[:],
@@ -179,11 +196,12 @@ def tile_heterogeneousgraphtransformer_pb_t_kernel(tc, att, scene_reps, Wo, bo, 
             if k >= PAIRS:
                 return
             sb_t[k] = sb_pool.tile([P, 2 * D], F32, name="sb%d" % k, tag="sb")
-            s0 = 2 * (k % 2) * D
+            att_tile, scene_tile, n, j0 = pair_load[k]
+            s0 = j0 * D
             for i in range(2):
                 engine.tensor_tensor(
                     out=sb_t[k][:, i * D:(i + 1) * D],
-                    in0=scene_t[k // 2][:, s0 + i * D:s0 + (i + 1) * D],
+                    in0=scene_tile[:, s0 + i * D:s0 + (i + 1) * D],
                     in1=bo_b[:],
                     op=ALU.add,
                 )
@@ -229,30 +247,56 @@ def tile_heterogeneousgraphtransformer_pb_t_kernel(tc, att, scene_reps, Wo, bo, 
                 out=o, in0=o, scalar=rstd_t[k][:, i:i + 1], in1=beta_ps[:], op0=ALU.mult, op1=ALU.add
             )
 
+        bo_ps = ps_const.tile([P, D], F32, name="bo_ps", tag="gamma")
+        nc.tensor.matmul(out=bo_ps[:], lhsT=ones[:], rhs=bo_row[:], start=True, stop=True)
+        bo_b = const.tile([P, D], BF16)
+        nc.vector.tensor_copy(out=bo_b[:], in_=bo_ps[:])
         transposes(0)
         regroup(0, 0)
         regroup(0, 1)
-        quantise(0)
-        gamma_ps = ps_const.tile([P, D], F32)
-        beta_ps = ps_const.tile([P, D], F32)
-        bo_ps = ps_xt.tile([P, D], F32, name="bo_ps", tag="xt")
-        nc.tensor.matmul(out=bo_ps[:], lhsT=ones[:], rhs=vecs[:, 0:D], start=True, stop=True)
-        nc.tensor.matmul(out=gamma_ps[:], lhsT=ones[:], rhs=vecs[:, D:2 * D], start=True, stop=True)
-        nc.tensor.matmul(out=beta_ps[:], lhsT=ones[:], rhs=vecs[:, 2 * D:3 * D], start=True, stop=True)
-        bo_b = const.tile([P, D], BF16)
-        nc.vector.tensor_copy(out=bo_b[:], in_=bo_ps[:])
         add_bias(0, nc.vector)
-        matmuls(0)
+        wo_transposes(0)
+        wo_transposes(1)
+        wo_regroup(0, 0, nc.vector.tensor_copy)
+        wo_regroup(0, 1, nc.scalar.copy)
+        quantise(0)
+        wo_regroup(1, 0, nc.vector.tensor_copy)
+        wo_regroup(1, 1, nc.scalar.copy)
+        for h in range(2):
+            for e in range(E):
+                wo_quantise(h, e)
+        gamma_ps = ps_const.tile([P, D], F32, name="gamma_ps", tag="gamma")
+        beta_ps = ps_const.tile([P, D], F32, name="beta_ps", tag="beta")
+        nc.tensor.matmul(out=gamma_ps[:], lhsT=ones[:], rhs=gb_rows[:, 0:D], start=True, stop=True)
+        nc.tensor.matmul(out=beta_ps[:], lhsT=ones[:], rhs=gb_rows[:, D:2 * D], start=True, stop=True)
         transposes(1)
         regroup(1, 0)
         regroup(1, 1)
-        quantise(1)
-        matmuls(1)
+        matmuls(0)
         transposes(2)
         add_bias(1, nc.gpsimd)
         add_bias(2, nc.gpsimd)
 
-        for n in range(PAIRS + 1):
+        residual(0, 0)
+        squares(0, 0)
+        residual(0, 1)
+        regroup(2, 0)
+        squares(0, 1)
+        regroup(2, 1)
+        inv_std(0)
+        quantise(1)
+        matmuls(1)
+        transposes(3)
+        regroup(3, 0)
+        regroup(3, 1)
+        centre_gain(0, 0)
+        centre_gain(0, 1)
+        quantise(2)
+        matmuls(2)
+        transposes(4)
+        add_bias(3, nc.gpsimd)
+
+        for n in range(1, PAIRS + 1):
             m = n - 1
             if n < PAIRS:
                 residual(n, 0)
@@ -260,23 +304,18 @@ def tile_heterogeneousgraphtransformer_pb_t_kernel(tc, att, scene_reps, Wo, bo, 
                 residual(n, 1)
                 squares(n, 1)
                 inv_std(n)
-                if n == 0:
-                    regroup(2, 0)
-                    regroup(2, 1)
-                    transposes(3)
                 regroup(n + 3, 0)
                 regroup(n + 3, 1)
-            if m >= 0:
-                scale_shift(m, 0)
-                if m == PAIRS - 1:
-                    nc.sync.dma_start(out=out_v[:, 2 * m, :], in_=o_t[m][:, 0:D])
-                scale_shift(m, 1)
-                if m == PAIRS - 1:
-                    nc.sync.dma_start(out=out_v[:, 2 * m + 1, :], in_=o_t[m][:, D:2 * D])
-                else:
-                    nc.sync.dma_start(
-                        out=out_v[:, 2 * m:2 * m + 2, :], in_=o_t[m][:].rearrange("p (j d) -> p j d", j=2)
-                    )
+            scale_shift(m, 0)
+            if m == PAIRS - 1:
+                nc.sync.dma_start(out=out_v[:, 2 * m, :], in_=o_t[m][:, 0:D])
+            scale_shift(m, 1)
+            if m == PAIRS - 1:
+                nc.sync.dma_start(out=out_v[:, 2 * m + 1, :], in_=o_t[m][:, D:2 * D])
+            else:
+                nc.sync.dma_start(
+                    out=out_v[:, 2 * m:2 * m + 2, :], in_=o_t[m][:].rearrange("p (j d) -> p j d", j=2)
+                )
             if n < PAIRS:
                 centre_gain(n, 0)
                 quantise(n + 2)

@@ -35,10 +35,12 @@ def tile_heterogeneousgraphtransformer_pb_t_kernel(tc, att, scene_reps, Wo, bo, 
         loads = ctx.enter_context(tc.tile_pool(name="loads", bufs=1))
         grp_pool = ctx.enter_context(tc.tile_pool(name="grp", bufs=3))
         code_pool = ctx.enter_context(tc.tile_pool(name="code", bufs=3))
-        sb_pool = ctx.enter_context(tc.tile_pool(name="sb", bufs=3))
+        sb_pool = ctx.enter_context(tc.tile_pool(name="sb", bufs=4))
+        zw_pool = ctx.enter_context(tc.tile_pool(name="zw", bufs=2))
         o_pool = ctx.enter_context(tc.tile_pool(name="o", bufs=10))
         small = ctx.enter_context(tc.tile_pool(name="small", bufs=4))
         ps_const = ctx.enter_context(tc.psum_pool(name="psc", bufs=1))
+        ps_zt = ctx.enter_context(tc.psum_pool(name="psz", bufs=1))
         ps_xt = ctx.enter_context(tc.psum_pool(name="psx", bufs=2))
         ps_f = ctx.enter_context(tc.psum_pool(name="psf", bufs=4))
         ctx.enter_context(tc.manual_schedule())
@@ -138,6 +140,10 @@ def tile_heterogeneousgraphtransformer_pb_t_kernel(tc, att, scene_reps, Wo, bo, 
         negmean_t = {}
         sumsq_t = {}
         rstd_t = {}
+        z_t = {}
+        zt_t = {}
+        w_t = {}
+        bk_t = {}
 
         def transposes(k):
             if k >= PAIRS:
@@ -192,15 +198,15 @@ def tile_heterogeneousgraphtransformer_pb_t_kernel(tc, att, scene_reps, Wo, bo, 
                         stop=(e == E - 1),
                     )
 
-        def add_bias(k, engine):
+        def add_bias(k, engine, order=(0, 1)):
             if k >= PAIRS:
                 return
-            sb_t[k] = sb_pool.tile([P, 2 * D], F32, name="sb%d" % k, tag="sb")
             att_tile, scene_tile, n, j0 = pair_load[k]
             s0 = j0 * D
-            for i in range(2):
+            for i in order:
+                sb_t[(k, i)] = sb_pool.tile([P, D], F32, name="sb%d_%d" % (k, i), tag="sb%d" % i, bufs=(4, 3)[i])
                 engine.tensor_tensor(
-                    out=sb_t[k][:, i * D:(i + 1) * D],
+                    out=sb_t[(k, i)][:],
                     in0=scene_tile[:, s0 + i * D:s0 + (i + 1) * D],
                     in1=bo_b[:],
                     op=ALU.add,
@@ -209,7 +215,7 @@ def tile_heterogeneousgraphtransformer_pb_t_kernel(tc, att, scene_reps, Wo, bo, 
         def residual(k, i):
             if i == 0:
                 sums_t[k] = small.tile([P, 2], F32, name="sums%d" % k, tag="sums")
-            y = sb_t[k][:, i * D:(i + 1) * D]
+            y = sb_t[(k, i)][:]
             nc.vector.scalar_tensor_tensor(
                 out=y, in0=y, scalar=1.0, in1=f_t[(k, i)][:], op0=ALU.mult, op1=ALU.add,
                 accum_out=sums_t[k][:, i:i + 1],
@@ -223,7 +229,7 @@ def tile_heterogeneousgraphtransformer_pb_t_kernel(tc, att, scene_reps, Wo, bo, 
                 out=negmean_t[k][:, i:i + 1], in_=sums_t[k][:, i:i + 1], func=ACT.Copy, scale=-1.0 / D
             )
             nc.scalar.activation(
-                out=squares_out[:], in_=sb_t[k][:, i * D:(i + 1) * D], func=ACT.Square,
+                out=squares_out[:], in_=sb_t[(k, i)][:], func=ACT.Square,
                 bias=negmean_t[k][:, i:i + 1], scale=1.0, accum_out=sumsq_t[k][:, i:i + 1],
             )
 
@@ -233,21 +239,61 @@ def tile_heterogeneousgraphtransformer_pb_t_kernel(tc, att, scene_reps, Wo, bo, 
                 out=rstd_t[k][:], in_=sumsq_t[k][:], func=ACT.Abs_reciprocal_sqrt, bias=eps_t[:], scale=1.0 / D
             )
 
-        def centre_gain(k, i):
-            if i == 0:
+        def out_tile(k):
+            if k not in o_t:
                 o_t[k] = o_pool.tile([P, 2 * D], F32, name="o%d" % k, tag="o")
+            return o_t[k]
+
+        def centre_gain(k, i):
             nc.vector.scalar_tensor_tensor(
-                out=o_t[k][:, i * D:(i + 1) * D], in0=sb_t[k][:, i * D:(i + 1) * D],
-                scalar=negmean_t[k][:, i:i + 1], in1=gamma_ps[:], op0=ALU.add, op1=ALU.mult,
+                out=out_tile(k)[:, i * D:(i + 1) * D], in0=sb_t[(k, i)][:],
+                scalar=negmean_t[k][:, i:i + 1], in1=gb_ps[:, 0:D], op0=ALU.add, op1=ALU.mult,
             )
 
         def scale_shift(k, i):
             o = o_t[k][:, i * D:(i + 1) * D]
             nc.vector.scalar_tensor_tensor(
-                out=o, in0=o, scalar=rstd_t[k][:, i:i + 1], in1=beta_ps[:], op0=ALU.mult, op1=ALU.add
+                out=o, in0=o, scalar=rstd_t[k][:, i:i + 1], in1=gb_ps[:, D:2 * D], op0=ALU.mult, op1=ALU.add
             )
 
-        bo_ps = ps_const.tile([P, D], F32, name="bo_ps", tag="gamma")
+        def turned(k):
+            return 0 < k < PAIRS - 2 and k % 2 == 0
+
+        def standardise(k):
+            z_t[k] = zw_pool.tile([P, D], F32, name="z%d" % k, tag="z")
+            nc.vector.tensor_scalar(
+                out=z_t[k][:], in0=sb_t[(k, 0)][:], scalar1=negmean_t[k][:, 0:1], scalar2=rstd_t[k][:, 0:1],
+                op0=ALU.add, op1=ALU.mult,
+            )
+
+        def turn(k):
+            zt_t[k] = ps_zt.tile([P, D], F32, name="zt%d" % k, tag="zt")
+            for b in range(D // P):
+                cols = slice(b * P, (b + 1) * P)
+                nc.tensor.transpose(out=zt_t[k][:, cols], in_=z_t[k][:, cols], identity=ident[:])
+
+        def gain_shift(k):
+            w_t[k] = zw_pool.tile([P, D], F32, name="w%d" % k, tag="w")
+            for b in range(D // P):
+                cols = slice(b * P, (b + 1) * P)
+                nc.scalar.activation(
+                    out=w_t[k][:, cols], in_=zt_t[k][:, cols], func=ACT.Identity,
+                    scale=gb_cols[:, b:b + 1], bias=gb_cols[:, D // P + b:D // P + b + 1],
+                )
+
+        def turn_back(k):
+            bk_t[k] = ps_zt.tile([P, D], F32, name="bk%d" % k, tag="zt")
+            for b in range(D // P):
+                cols = slice(b * P, (b + 1) * P)
+                nc.tensor.transpose(out=bk_t[k][:, cols], in_=w_t[k][:, cols], identity=ident[:])
+
+        def copy_out(k):
+            nc.scalar.copy(out=out_tile(k)[:, 0:D], in_=bk_t[k][:])
+
+        def store(k):
+            nc.sync.dma_start(out=out_v[:, 2 * k:2 * k + 2, :], in_=o_t[k][:].rearrange("p (j d) -> p j d", j=2))
+
+        bo_ps = ps_zt.tile([P, D], F32, name="bo_ps", tag="zt")
         nc.tensor.matmul(out=bo_ps[:], lhsT=ones[:], rhs=bo_row[:], start=True, stop=True)
         bo_b = const.tile([P, D], BF16)
         nc.vector.tensor_copy(out=bo_b[:], in_=bo_ps[:])
@@ -265,10 +311,17 @@ def tile_heterogeneousgraphtransformer_pb_t_kernel(tc, att, scene_reps, Wo, bo, 
         for h in range(2):
             for e in range(E):
                 wo_quantise(h, e)
-        gamma_ps = ps_const.tile([P, D], F32, name="gamma_ps", tag="gamma")
-        beta_ps = ps_const.tile([P, D], F32, name="beta_ps", tag="beta")
-        nc.tensor.matmul(out=gamma_ps[:], lhsT=ones[:], rhs=gb_rows[:, 0:D], start=True, stop=True)
-        nc.tensor.matmul(out=beta_ps[:], lhsT=ones[:], rhs=gb_rows[:, D:2 * D], start=True, stop=True)
+        gb_ps = ps_const.tile([P, 2 * D], BF16)
+        for v in range(2):
+            nc.tensor.matmul(
+                out=gb_ps[:, v * D:(v + 1) * D], lhsT=ones[:], rhs=gb_rows[:, v * D:(v + 1) * D], start=True, stop=True
+            )
+        cols_ps = ps_zt.tile([P, D], F32, name="cols_ps", tag="zt")
+        for b in range(2 * D // P):
+            nc.tensor.matmul(
+                out=cols_ps[:, b:b + 1], lhsT=gb_rows[:, b * P:(b + 1) * P], rhs=ones[:, 0:1], start=True, stop=True
+            )
+        gb_cols = const.tile([P, 2 * D // P], F32)
         transposes(1)
         regroup(1, 0)
         regroup(1, 1)
@@ -291,10 +344,11 @@ def tile_heterogeneousgraphtransformer_pb_t_kernel(tc, att, scene_reps, Wo, bo, 
         regroup(3, 1)
         centre_gain(0, 0)
         centre_gain(0, 1)
+        nc.vector.tensor_copy(out=gb_cols[:], in_=cols_ps[:, 0:2 * D // P])
         quantise(2)
         matmuls(2)
         transposes(4)
-        add_bias(3, nc.gpsimd)
+        add_bias(3, nc.gpsimd, (1, 0))
 
         for n in range(1, PAIRS + 1):
             m = n - 1
@@ -304,22 +358,31 @@ def tile_heterogeneousgraphtransformer_pb_t_kernel(tc, att, scene_reps, Wo, bo, 
                 residual(n, 1)
                 squares(n, 1)
                 inv_std(n)
-                regroup(n + 3, 0)
-                regroup(n + 3, 1)
-            scale_shift(m, 0)
+            if turned(n - 2):
+                copy_out(n - 2)
+                store(n - 2)
+            regroup(n + 3, 0)
+            regroup(n + 3, 1)
+            if not turned(m):
+                scale_shift(m, 0)
             if m == PAIRS - 1:
                 nc.sync.dma_start(out=out_v[:, 2 * m, :], in_=o_t[m][:, 0:D])
             scale_shift(m, 1)
             if m == PAIRS - 1:
                 nc.sync.dma_start(out=out_v[:, 2 * m + 1, :], in_=o_t[m][:, D:2 * D])
-            else:
-                nc.sync.dma_start(
-                    out=out_v[:, 2 * m:2 * m + 2, :], in_=o_t[m][:].rearrange("p (j d) -> p j d", j=2)
-                )
+            elif not turned(m):
+                store(m)
             if n < PAIRS:
-                centre_gain(n, 0)
+                if not turned(n):
+                    centre_gain(n, 0)
+                if turned(m):
+                    standardise(m)
+                    turn(m)
+                    gain_shift(m)
                 quantise(n + 2)
                 matmuls(n + 2)
+                if turned(m):
+                    turn_back(m)
                 transposes(n + 4)
                 centre_gain(n, 1)
-                add_bias(n + 3, nc.gpsimd)
+                add_bias(n + 3, nc.gpsimd, (1, 0))

@@ -20,6 +20,7 @@ PAIRS = TILES // 2
 LOAD_TILES = (2, 2) + (4,) * ((TILES - 4) // 4)
 WORDS = D // 2
 EPS = 1e-5
+RING = 6
 FLOPS = 2 * TOKENS * E * D * D
 
 
@@ -33,9 +34,8 @@ def tile_heterogeneousgraphtransformer_pb_t_kernel(tc, att, scene_reps, Wo, bo, 
     with ExitStack() as ctx:
         const = ctx.enter_context(tc.tile_pool(name="const", bufs=1))
         loads = ctx.enter_context(tc.tile_pool(name="loads", bufs=1))
-        grp_pool = ctx.enter_context(tc.tile_pool(name="grp", bufs=3))
+        ring_pool = ctx.enter_context(tc.tile_pool(name="ring", bufs=1))
         code_pool = ctx.enter_context(tc.tile_pool(name="code", bufs=3))
-        sb_pool = ctx.enter_context(tc.tile_pool(name="sb", bufs=4))
         zw_pool = ctx.enter_context(tc.tile_pool(name="zw", bufs=2))
         o_pool = ctx.enter_context(tc.tile_pool(name="o", bufs=10))
         small = ctx.enter_context(tc.tile_pool(name="small", bufs=4))
@@ -166,7 +166,7 @@ def tile_heterogeneousgraphtransformer_pb_t_kernel(tc, att, scene_reps, Wo, bo, 
             if k >= PAIRS:
                 return
             if i == 0:
-                grp_t[k] = grp_pool.tile([P, 2 * E * P * 4], BF16, name="grp%d" % k, tag="grp", align_bytes=64)
+                grp_t[k] = ring_pool.tile([P, 2 * E * P * 4], BF16, name="grp%d" % k, tag="ring%d" % (k % RING), align_bytes=64)
             g_f = grp_t[k][:].bitcast(F32)
             nc.scalar.copy(
                 out=g_f[:, i * D:(i + 1) * D].rearrange("p (e r u) -> p e r u", e=E, u=2),
@@ -198,38 +198,37 @@ def tile_heterogeneousgraphtransformer_pb_t_kernel(tc, att, scene_reps, Wo, bo, 
                         stop=(e == E - 1),
                     )
 
-        def add_bias(k, engine, order=(0, 1)):
+        def add_bias(k, engine):
             if k >= PAIRS:
                 return
+            sb_t[k] = ring_pool.tile(
+                [P, 2 * D], F32, name="sb%d" % k, tag="ring%d" % ((k - 1) % RING), align_bytes=64)
             att_tile, scene_tile, n, j0 = pair_load[k]
-            s0 = j0 * D
-            for i in order:
-                sb_t[(k, i)] = sb_pool.tile([P, D], F32, name="sb%d_%d" % (k, i), tag="sb%d" % i, bufs=(4, 3)[i])
-                engine.tensor_tensor(
-                    out=sb_t[(k, i)][:],
-                    in0=scene_tile[:, s0 + i * D:s0 + (i + 1) * D],
-                    in1=bo_b[:],
-                    op=ALU.add,
-                )
+            engine.tensor_tensor(
+                out=sb_t[k][:].rearrange("p (j d) -> p j d", j=2),
+                in0=scene_tile[:, j0 * D:(j0 + 2) * D].rearrange("p (j d) -> p j d", j=2),
+                in1=bo_b[:].unsqueeze(1).to_broadcast([P, 2, D]),
+                op=ALU.add,
+            )
 
         def residual(k, i):
             if i == 0:
                 sums_t[k] = small.tile([P, 2], F32, name="sums%d" % k, tag="sums")
-            y = sb_t[(k, i)][:]
+            y = sb_t[k][:, i * D:(i + 1) * D]
             nc.vector.scalar_tensor_tensor(
                 out=y, in0=y, scalar=1.0, in1=f_t[(k, i)][:], op0=ALU.mult, op1=ALU.add,
                 accum_out=sums_t[k][:, i:i + 1],
             )
 
+        def neg_mean(k):
+            negmean_t[k] = small.tile([P, 2], F32, name="negmean%d" % k, tag="negmean")
+            nc.scalar.activation(out=negmean_t[k][:], in_=sums_t[k][:], func=ACT.Copy, scale=-1.0 / D)
+
         def squares(k, i):
             if i == 0:
-                negmean_t[k] = small.tile([P, 2], F32, name="negmean%d" % k, tag="negmean")
                 sumsq_t[k] = small.tile([P, 2], F32, name="sumsq%d" % k, tag="sumsq")
             nc.scalar.activation(
-                out=negmean_t[k][:, i:i + 1], in_=sums_t[k][:, i:i + 1], func=ACT.Copy, scale=-1.0 / D
-            )
-            nc.scalar.activation(
-                out=squares_out[:], in_=sb_t[(k, i)][:], func=ACT.Square,
+                out=squares_out[:], in_=sb_t[k][:, i * D:(i + 1) * D], func=ACT.Square,
                 bias=negmean_t[k][:, i:i + 1], scale=1.0, accum_out=sumsq_t[k][:, i:i + 1],
             )
 
@@ -246,7 +245,7 @@ def tile_heterogeneousgraphtransformer_pb_t_kernel(tc, att, scene_reps, Wo, bo, 
 
         def centre_gain(k, i):
             nc.vector.scalar_tensor_tensor(
-                out=out_tile(k)[:, i * D:(i + 1) * D], in0=sb_t[(k, i)][:],
+                out=out_tile(k)[:, i * D:(i + 1) * D], in0=sb_t[k][:, i * D:(i + 1) * D],
                 scalar=negmean_t[k][:, i:i + 1], in1=gb_ps[:, 0:D], op0=ALU.add, op1=ALU.mult,
             )
 
@@ -262,7 +261,7 @@ def tile_heterogeneousgraphtransformer_pb_t_kernel(tc, att, scene_reps, Wo, bo, 
         def standardise(k):
             z_t[k] = zw_pool.tile([P, D], F32, name="z%d" % k, tag="z")
             nc.vector.tensor_scalar(
-                out=z_t[k][:], in0=sb_t[(k, 0)][:], scalar1=negmean_t[k][:, 0:1], scalar2=rstd_t[k][:, 0:1],
+                out=z_t[k][:], in0=sb_t[k][:, 0:D], scalar1=negmean_t[k][:, 0:1], scalar2=rstd_t[k][:, 0:1],
                 op0=ALU.add, op1=ALU.mult,
             )
 
@@ -328,16 +327,17 @@ def tile_heterogeneousgraphtransformer_pb_t_kernel(tc, att, scene_reps, Wo, bo, 
         matmuls(0)
         transposes(2)
         add_bias(1, nc.gpsimd)
-        add_bias(2, nc.gpsimd)
 
         residual(0, 0)
-        squares(0, 0)
         residual(0, 1)
         regroup(2, 0)
-        squares(0, 1)
+        neg_mean(0)
+        squares(0, 0)
         regroup(2, 1)
+        squares(0, 1)
         inv_std(0)
         quantise(1)
+        add_bias(2, nc.gpsimd)
         matmuls(1)
         transposes(3)
         regroup(3, 0)
@@ -348,21 +348,23 @@ def tile_heterogeneousgraphtransformer_pb_t_kernel(tc, att, scene_reps, Wo, bo, 
         quantise(2)
         matmuls(2)
         transposes(4)
-        add_bias(3, nc.gpsimd, (1, 0))
+        add_bias(3, nc.gpsimd)
 
         for n in range(1, PAIRS + 1):
             m = n - 1
             if n < PAIRS:
                 residual(n, 0)
-                squares(n, 0)
                 residual(n, 1)
+                regroup(n + 3, 0)
+                regroup(n + 3, 1)
+                transposes(n + 4)
+                neg_mean(n)
+                squares(n, 0)
                 squares(n, 1)
                 inv_std(n)
             if turned(n - 2):
                 copy_out(n - 2)
                 store(n - 2)
-            regroup(n + 3, 0)
-            regroup(n + 3, 1)
             if not turned(m):
                 scale_shift(m, 0)
             if m == PAIRS - 1:
@@ -380,9 +382,8 @@ def tile_heterogeneousgraphtransformer_pb_t_kernel(tc, att, scene_reps, Wo, bo, 
                     turn(m)
                     gain_shift(m)
                 quantise(n + 2)
+                add_bias(n + 3, nc.gpsimd)
                 matmuls(n + 2)
                 if turned(m):
                     turn_back(m)
-                transposes(n + 4)
                 centre_gain(n, 1)
-                add_bias(n + 3, nc.gpsimd, (1, 0))

@@ -55,7 +55,7 @@ def tile_heterogeneousgraphtransformer_pb_t_kernel(tc, att, scene_reps, Wo, bo, 
         nc.vector.memset(gb_rows[:].bitcast(U32), 0)
         eps_t = const.tile([P, 1], F32)
         nc.vector.memset(eps_t[:], EPS)
-        squares_out = const.tile([P, D], F32)
+        squares_out = const.tile([P, 2 * D], F32)
 
         nc.sync.dma_start(out=bo_row[0:1, :], in_=bo.rearrange("(o d) -> o d", o=1))
         for i, v in enumerate((gamma, beta)):
@@ -140,6 +140,7 @@ def tile_heterogeneousgraphtransformer_pb_t_kernel(tc, att, scene_reps, Wo, bo, 
         negmean_t = {}
         sumsq_t = {}
         rstd_t = {}
+        shift_t = {}
         z_t = {}
         zt_t = {}
         w_t = {}
@@ -228,14 +229,16 @@ def tile_heterogeneousgraphtransformer_pb_t_kernel(tc, att, scene_reps, Wo, bo, 
             if i == 0:
                 sumsq_t[k] = small.tile([P, 2], F32, name="sumsq%d" % k, tag="sumsq")
             nc.scalar.activation(
-                out=squares_out[:], in_=sb_t[k][:, i * D:(i + 1) * D], func=ACT.Square,
+                out=squares_out[:, i * D:(i + 1) * D], in_=sb_t[k][:, i * D:(i + 1) * D], func=ACT.Square,
                 bias=negmean_t[k][:, i:i + 1], scale=1.0, accum_out=sumsq_t[k][:, i:i + 1],
             )
 
-        def inv_std(k):
-            rstd_t[k] = small.tile([P, 2], F32, name="rstd%d" % k, tag="rstd")
+        def inv_std(k, i=0, n=2):
+            if k not in rstd_t:
+                rstd_t[k] = small.tile([P, 2], F32, name="rstd%d" % k, tag="rstd")
             nc.scalar.activation(
-                out=rstd_t[k][:], in_=sumsq_t[k][:], func=ACT.Abs_reciprocal_sqrt, bias=eps_t[:], scale=1.0 / D
+                out=rstd_t[k][:, i:i + n], in_=sumsq_t[k][:, i:i + n], func=ACT.Abs_reciprocal_sqrt, bias=eps_t[:],
+                scale=1.0 / D,
             )
 
         def out_tile(k):
@@ -255,15 +258,32 @@ def tile_heterogeneousgraphtransformer_pb_t_kernel(tc, att, scene_reps, Wo, bo, 
                 out=o, in0=o, scalar=rstd_t[k][:, i:i + 1], in1=gb_ps[:, D:2 * D], op0=ALU.mult, op1=ALU.add
             )
 
-        def turned(k):
-            return 0 < k < PAIRS - 2 and k % 2 == 0
+        def late(k):
+            return k >= PAIRS - 3
+
+        def on_gpsimd(k):
+            return late(k) and k < PAIRS - 1
+
+        def neg_mean_rstd(k):
+            shift_t[k] = small.tile([P, 1], F32, name="shift%d" % k, tag="shift")
+            nc.scalar.activation(
+                out=shift_t[k][:], in_=negmean_t[k][:, 0:1], func=ACT.Copy, scale=rstd_t[k][:, 0:1]
+            )
 
         def standardise(k):
             z_t[k] = zw_pool.tile([P, D], F32, name="z%d" % k, tag="z")
-            nc.vector.tensor_scalar(
-                out=z_t[k][:], in0=sb_t[k][:, 0:D], scalar1=negmean_t[k][:, 0:1], scalar2=rstd_t[k][:, 0:1],
-                op0=ALU.add, op1=ALU.mult,
+            nc.scalar.activation(
+                out=z_t[k][:], in_=sb_t[k][:, 0:D], func=ACT.Identity, scale=rstd_t[k][:, 0:1], bias=shift_t[k][:]
             )
+
+        def gain_shift_gpsimd(k):
+            o = out_tile(k)[:, 0:D]
+            w = zw_pool.tile([P, D], F32, name="w%d" % k, tag="w")
+            nc.gpsimd.tensor_tensor(out=w[:], in0=z_t[k][:], in1=gb_sb[:, 0:D], op=ALU.mult)
+            nc.gpsimd.tensor_tensor(out=o, in0=w[:], in1=gb_sb[:, D:2 * D], op=ALU.add)
+
+        def turned(k):
+            return 0 < k < PAIRS - 4 and k % 2 == 1
 
         def turn(k):
             zt_t[k] = ps_zt.tile([P, D], F32, name="zt%d" % k, tag="zt")
@@ -288,6 +308,9 @@ def tile_heterogeneousgraphtransformer_pb_t_kernel(tc, att, scene_reps, Wo, bo, 
 
         def copy_out(k):
             nc.scalar.copy(out=out_tile(k)[:, 0:D], in_=bk_t[k][:])
+
+        def store_tile(k, i):
+            nc.sync.dma_start(out=out_v[:, 2 * k + i, :], in_=o_t[k][:, i * D:(i + 1) * D])
 
         def store(k):
             nc.sync.dma_start(out=out_v[:, 2 * k:2 * k + 2, :], in_=o_t[k][:].rearrange("p (j d) -> p j d", j=2))
@@ -321,6 +344,8 @@ def tile_heterogeneousgraphtransformer_pb_t_kernel(tc, att, scene_reps, Wo, bo, 
                 out=cols_ps[:, b:b + 1], lhsT=gb_rows[:, b * P:(b + 1) * P], rhs=ones[:, 0:1], start=True, stop=True
             )
         gb_cols = const.tile([P, 2 * D // P], F32)
+        gb_sb = const.tile([P, 2 * D], BF16)
+        nc.vector.tensor_copy(out=gb_sb[:], in_=gb_ps[:])
         transposes(1)
         regroup(1, 0)
         regroup(1, 1)
@@ -332,22 +357,22 @@ def tile_heterogeneousgraphtransformer_pb_t_kernel(tc, att, scene_reps, Wo, bo, 
         residual(0, 1)
         regroup(2, 0)
         neg_mean(0)
-        squares(0, 0)
         regroup(2, 1)
+        squares(0, 0)
         squares(0, 1)
-        inv_std(0)
         quantise(1)
         add_bias(2, nc.gpsimd)
         matmuls(1)
         transposes(3)
         regroup(3, 0)
         regroup(3, 1)
+        inv_std(0)
         centre_gain(0, 0)
         centre_gain(0, 1)
         nc.vector.tensor_copy(out=gb_cols[:], in_=cols_ps[:, 0:2 * D // P])
         quantise(2)
-        matmuls(2)
         transposes(4)
+        matmuls(2)
         add_bias(3, nc.gpsimd)
 
         for n in range(1, PAIRS + 1):
@@ -356,30 +381,45 @@ def tile_heterogeneousgraphtransformer_pb_t_kernel(tc, att, scene_reps, Wo, bo, 
                 residual(n, 0)
                 residual(n, 1)
                 regroup(n + 3, 0)
+                if turned(m):
+                    neg_mean_rstd(m)
+                neg_mean(n)
+                if turned(m):
+                    standardise(m)
                 regroup(n + 3, 1)
                 transposes(n + 4)
-                neg_mean(n)
+                if turned(m):
+                    turn(m)
                 squares(n, 0)
+                if late(n):
+                    inv_std(n, 0, 1)
                 squares(n, 1)
-                inv_std(n)
+                if on_gpsimd(n):
+                    neg_mean_rstd(n)
+                if late(n):
+                    inv_std(n, 1, 1)
+                if on_gpsimd(n):
+                    standardise(n)
+                    gain_shift_gpsimd(n)
             if turned(n - 2):
                 copy_out(n - 2)
                 store(n - 2)
-            if not turned(m):
+            if not late(n):
+                inv_std(n)
+            if not turned(m) and not on_gpsimd(m):
                 scale_shift(m, 0)
             if m == PAIRS - 1:
-                nc.sync.dma_start(out=out_v[:, 2 * m, :], in_=o_t[m][:, 0:D])
+                store_tile(m - 1, 0)
+                store_tile(m, 0)
             scale_shift(m, 1)
-            if m == PAIRS - 1:
-                nc.sync.dma_start(out=out_v[:, 2 * m + 1, :], in_=o_t[m][:, D:2 * D])
+            if m >= PAIRS - 2:
+                store_tile(m, 1)
             elif not turned(m):
                 store(m)
             if n < PAIRS:
-                if not turned(n):
+                if not turned(n) and not on_gpsimd(n):
                     centre_gain(n, 0)
                 if turned(m):
-                    standardise(m)
-                    turn(m)
                     gain_shift(m)
                 quantise(n + 2)
                 add_bias(n + 3, nc.gpsimd)

@@ -20,7 +20,7 @@ PAIRS = TILES // 2
 LOAD_TILES = (2, 2) + (4,) * ((TILES - 4) // 4)
 WORDS = D // 2
 EPS = 1e-5
-RING = 6
+RING = 5
 FLOPS = 2 * TOKENS * E * D * D
 
 
@@ -47,19 +47,22 @@ def tile_heterogeneousgraphtransformer_pb_t_kernel(tc, att, scene_reps, Wo, bo, 
 
         ident = const.tile([P, P], F32)
         make_identity(nc, ident[:])
+        ones = const.tile([P, D], BF16)
+        nc.vector.memset(ones[:], 1.0)
         bo_row = const.tile([P, D], BF16)
         nc.vector.memset(bo_row[:].bitcast(U32), 0)
-        ones = const.tile([P, P], BF16)
-        nc.vector.memset(ones[:], 1.0)
+
+        def warm_up(n):
+            scratch = ps_zt.tile([P, D], F32, name="scratch%d" % n, tag="zt")
+            for i in range(n):
+                nc.tensor.matmul(out=scratch[:], lhsT=ones[:, 0:P], rhs=ones[:], start=True, stop=True)
+
         gb_rows = const.tile([P, 2 * D], BF16)
         nc.vector.memset(gb_rows[:].bitcast(U32), 0)
         eps_t = const.tile([P, 1], F32)
         nc.vector.memset(eps_t[:], EPS)
         squares_out = const.tile([P, 2 * D], F32)
 
-        nc.sync.dma_start(out=bo_row[0:1, :], in_=bo.rearrange("(o d) -> o d", o=1))
-        for i, v in enumerate((gamma, beta)):
-            nc.scalar.dma_start(out=gb_rows[0:1, i * D:(i + 1) * D], in_=v.rearrange("(o d) -> o d", o=1))
         warm = const.tile([P, 1], F32)
         nc.scalar.activation(out=warm[:], in_=eps_t[:], func=ACT.Abs_reciprocal_sqrt)
 
@@ -84,11 +87,14 @@ def tile_heterogeneousgraphtransformer_pb_t_kernel(tc, att, scene_reps, Wo, bo, 
         for h in range(2):
             wo_sb.append(const.tile([P, 2 * E * D], BF16, name="wo%d" % h))
         load_att(0)
-        load_scene(0)
+        nc.sync.dma_start(out=bo_row[0:1, :], in_=bo.rearrange("(o d) -> o d", o=1))
+        for i, v in enumerate((gamma, beta)):
+            nc.sync.dma_start(out=gb_rows[0:1, i * D:(i + 1) * D], in_=v.rearrange("(o d) -> o d", o=1))
         for h in range(2):
             nc.sync.dma_start(
                 out=wo_sb[h][:].rearrange("p (t k) -> p t k", t=2), in_=wo_v[:, 2 * h:2 * h + 2, :],
             )
+        load_scene(0)
         load_att(1)
         load_scene(1)
         for c in range(2, len(LOAD_TILES)):
@@ -203,7 +209,7 @@ def tile_heterogeneousgraphtransformer_pb_t_kernel(tc, att, scene_reps, Wo, bo, 
             if k >= PAIRS:
                 return
             sb_t[k] = ring_pool.tile(
-                [P, 2 * D], F32, name="sb%d" % k, tag="ring%d" % ((k - 1) % RING), align_bytes=64)
+                [P, 2 * D], F32, name="sb%d" % k, tag="ring%d" % (k % RING), align_bytes=64)
             att_tile, scene_tile, n, j0 = pair_load[k]
             engine.tensor_tensor(
                 out=sb_t[k][:].rearrange("p (j d) -> p j d", j=2),
@@ -315,28 +321,22 @@ def tile_heterogeneousgraphtransformer_pb_t_kernel(tc, att, scene_reps, Wo, bo, 
         def store(k):
             nc.sync.dma_start(out=out_v[:, 2 * k:2 * k + 2, :], in_=o_t[k][:].rearrange("p (j d) -> p j d", j=2))
 
-        bo_ps = ps_zt.tile([P, D], F32, name="bo_ps", tag="zt")
-        nc.tensor.matmul(out=bo_ps[:], lhsT=ones[:], rhs=bo_row[:], start=True, stop=True)
-        bo_b = const.tile([P, D], BF16)
-        nc.vector.tensor_copy(out=bo_b[:], in_=bo_ps[:])
+        warm_up(4)
         transposes(0)
         regroup(0, 0)
         regroup(0, 1)
-        add_bias(0, nc.vector)
+        quantise(0)
+        warm_up(2)
+        bo_ps = ps_zt.tile([P, D], F32, name="bo_ps", tag="zt")
+        nc.tensor.matmul(out=bo_ps[:], lhsT=ones[:, 0:P], rhs=bo_row[:], start=True, stop=True)
+        bo_b = const.tile([P, D], BF16)
+        nc.scalar.copy(out=bo_b[:], in_=bo_ps[:])
         wo_transposes(0)
         wo_transposes(1)
-        wo_regroup(0, 0, nc.vector.tensor_copy)
-        wo_regroup(0, 1, nc.scalar.copy)
-        quantise(0)
-        wo_regroup(1, 0, nc.vector.tensor_copy)
-        wo_regroup(1, 1, nc.scalar.copy)
-        for h in range(2):
-            for e in range(E):
-                wo_quantise(h, e)
         gb_ps = ps_const.tile([P, 2 * D], BF16)
         for v in range(2):
             nc.tensor.matmul(
-                out=gb_ps[:, v * D:(v + 1) * D], lhsT=ones[:], rhs=gb_rows[:, v * D:(v + 1) * D], start=True, stop=True
+                out=gb_ps[:, v * D:(v + 1) * D], lhsT=ones[:, 0:P], rhs=gb_rows[:, v * D:(v + 1) * D], start=True, stop=True
             )
         cols_ps = ps_zt.tile([P, D], F32, name="cols_ps", tag="zt")
         for b in range(2 * D // P):
@@ -344,36 +344,43 @@ def tile_heterogeneousgraphtransformer_pb_t_kernel(tc, att, scene_reps, Wo, bo, 
                 out=cols_ps[:, b:b + 1], lhsT=gb_rows[:, b * P:(b + 1) * P], rhs=ones[:, 0:1], start=True, stop=True
             )
         gb_cols = const.tile([P, 2 * D // P], F32)
-        gb_sb = const.tile([P, 2 * D], BF16)
-        nc.vector.tensor_copy(out=gb_sb[:], in_=gb_ps[:])
+        wo_regroup(0, 0, nc.vector.tensor_copy)
+        wo_regroup(0, 1, nc.scalar.copy)
+        wo_regroup(1, 0, nc.vector.tensor_copy)
+        wo_regroup(1, 1, nc.scalar.copy)
+        for e in range(E):
+            for h in range(2):
+                wo_quantise(h, e)
         transposes(1)
+        gb_sb = const.tile([P, 2 * D], BF16)
         regroup(1, 0)
         regroup(1, 1)
+        add_bias(0, nc.vector)
         matmuls(0)
-        transposes(2)
+        quantise(1)
         add_bias(1, nc.gpsimd)
+        transposes(2)
+        matmuls(1)
 
         residual(0, 0)
         residual(0, 1)
         regroup(2, 0)
         neg_mean(0)
         regroup(2, 1)
+        transposes(3)
         squares(0, 0)
         squares(0, 1)
-        quantise(1)
-        add_bias(2, nc.gpsimd)
-        matmuls(1)
-        transposes(3)
         regroup(3, 0)
         regroup(3, 1)
         inv_std(0)
         centre_gain(0, 0)
         centre_gain(0, 1)
         nc.vector.tensor_copy(out=gb_cols[:], in_=cols_ps[:, 0:2 * D // P])
+        nc.vector.tensor_copy(out=gb_sb[:], in_=gb_ps[:])
         quantise(2)
         transposes(4)
         matmuls(2)
-        add_bias(3, nc.gpsimd)
+        add_bias(2, nc.gpsimd)
 
         for n in range(1, PAIRS + 1):
             m = n - 1
@@ -400,7 +407,6 @@ def tile_heterogeneousgraphtransformer_pb_t_kernel(tc, att, scene_reps, Wo, bo, 
                     inv_std(n, 1, 1)
                 if on_gpsimd(n):
                     standardise(n)
-                    gain_shift_gpsimd(n)
             if turned(n - 2):
                 copy_out(n - 2)
                 store(n - 2)
@@ -422,8 +428,10 @@ def tile_heterogeneousgraphtransformer_pb_t_kernel(tc, att, scene_reps, Wo, bo, 
                 if turned(m):
                     gain_shift(m)
                 quantise(n + 2)
-                add_bias(n + 3, nc.gpsimd)
+                add_bias(n + 2, nc.gpsimd)
                 matmuls(n + 2)
+                if on_gpsimd(n):
+                    gain_shift_gpsimd(n)
                 if turned(m):
                     turn_back(m)
                 centre_gain(n, 1)

@@ -47,10 +47,10 @@ def tile_heterogeneousgraphtransformer_pb_t_kernel(tc, att, scene_reps, Wo, bo, 
 
         ident = const.tile([P, P], F32)
         make_identity(nc, ident[:])
-        ones = const.tile([P, D], BF16)
-        nc.vector.memset(ones[:], 1.0)
         bo_row = const.tile([P, D], BF16)
         nc.vector.memset(bo_row[:].bitcast(U32), 0)
+        ones = const.tile([P, D], BF16)
+        nc.vector.memset(ones[:], 1.0)
 
         def warm_up(n):
             scratch = ps_zt.tile([P, D], F32, name="scratch%d" % n, tag="zt")
@@ -84,16 +84,16 @@ def tile_heterogeneousgraphtransformer_pb_t_kernel(tc, att, scene_reps, Wo, bo, 
             nc.sync.dma_start(out=scene_t[c][:].rearrange("p (j d) -> p j d", j=n), in_=scene_v[:, g:g + n, :])
 
         wo_sb = []
-        for h in range(2):
-            wo_sb.append(const.tile([P, 2 * E * D], BF16, name="wo%d" % h))
-        load_att(0)
+        for t in range(4):
+            wo_sb.append(const.tile([P, E * D], BF16, name="wo%d" % t))
+        for t in range(0, 1):
+            nc.sync.dma_start(out=wo_sb[t][:], in_=wo_v[:, t, :])
         nc.sync.dma_start(out=bo_row[0:1, :], in_=bo.rearrange("(o d) -> o d", o=1))
         for i, v in enumerate((gamma, beta)):
             nc.sync.dma_start(out=gb_rows[0:1, i * D:(i + 1) * D], in_=v.rearrange("(o d) -> o d", o=1))
-        for h in range(2):
-            nc.sync.dma_start(
-                out=wo_sb[h][:].rearrange("p (t k) -> p t k", t=2), in_=wo_v[:, 2 * h:2 * h + 2, :],
-            )
+        for t in range(1, 4):
+            nc.sync.dma_start(out=wo_sb[t][:], in_=wo_v[:, t, :])
+        load_att(0)
         load_scene(0)
         load_att(1)
         load_scene(1)
@@ -108,16 +108,15 @@ def tile_heterogeneousgraphtransformer_pb_t_kernel(tc, att, scene_reps, Wo, bo, 
         wt_t = {}
 
         def wo_transposes(h):
-            wo_f = wo_sb[h][:].bitcast(F32)
             for e in range(E):
-                wt = ps_f.tile([P, D], F32, name="wt%d%d" % (h, e), tag="f")
-                wt_t[(h, e)] = wt
-                for t in range(2):
+                wt_t[(h, e)] = ps_f.tile([P, D], F32, name="wt%d%d" % (h, e), tag="f")
+            for t in range(2):
+                wo_f = wo_sb[2 * h + t][:].bitcast(F32)
+                for e in range(E):
                     for u in range(2):
-                        w0 = (t * E + e) * WORDS
                         nc.tensor.transpose(
-                            out=wt[:, (t * 2 + u) * P:(t * 2 + u + 1) * P], in_=wo_f[:, w0 + u:w0 + WORDS:2],
-                            identity=ident[:],
+                            out=wt_t[(h, e)][:, (t * 2 + u) * P:(t * 2 + u + 1) * P],
+                            in_=wo_f[:, e * WORDS + u:(e + 1) * WORDS:2], identity=ident[:],
                         )
 
         def wo_regroup(h, e, copy):
@@ -169,13 +168,13 @@ def tile_heterogeneousgraphtransformer_pb_t_kernel(tc, att, scene_reps, Wo, bo, 
                             identity=ident[:],
                         )
 
-        def regroup(k, i):
+        def regroup(k, i, copy=nc.scalar.copy):
             if k >= PAIRS:
                 return
             if i == 0:
                 grp_t[k] = ring_pool.tile([P, 2 * E * P * 4], BF16, name="grp%d" % k, tag="ring%d" % (k % RING), align_bytes=64)
             g_f = grp_t[k][:].bitcast(F32)
-            nc.scalar.copy(
+            copy(
                 out=g_f[:, i * D:(i + 1) * D].rearrange("p (e r u) -> p e r u", e=E, u=2),
                 in_=xt_t[(k, i)][:].rearrange("p (e u r) -> p e r u", e=E, u=2),
             )
@@ -322,41 +321,42 @@ def tile_heterogeneousgraphtransformer_pb_t_kernel(tc, att, scene_reps, Wo, bo, 
             nc.sync.dma_start(out=out_v[:, 2 * k:2 * k + 2, :], in_=o_t[k][:].rearrange("p (j d) -> p j d", j=2))
 
         warm_up(4)
-        transposes(0)
-        regroup(0, 0)
-        regroup(0, 1)
-        quantise(0)
-        warm_up(2)
         bo_ps = ps_zt.tile([P, D], F32, name="bo_ps", tag="zt")
         nc.tensor.matmul(out=bo_ps[:], lhsT=ones[:, 0:P], rhs=bo_row[:], start=True, stop=True)
         bo_b = const.tile([P, D], BF16)
         nc.scalar.copy(out=bo_b[:], in_=bo_ps[:])
         wo_transposes(0)
-        wo_transposes(1)
+        wo_regroup(0, 0, nc.vector.tensor_copy)
+        wo_regroup(0, 1, nc.scalar.copy)
         gb_ps = ps_const.tile([P, 2 * D], BF16)
         for v in range(2):
             nc.tensor.matmul(
                 out=gb_ps[:, v * D:(v + 1) * D], lhsT=ones[:, 0:P], rhs=gb_rows[:, v * D:(v + 1) * D], start=True, stop=True
             )
+        wo_transposes(1)
+        wo_quantise(0, 0)
+        wo_regroup(1, 0, nc.vector.tensor_copy)
+        wo_regroup(1, 1, nc.scalar.copy)
+        transposes(0)
+        regroup(0, 0, nc.scalar.copy)
+        wo_quantise(0, 1)
+        wo_quantise(1, 0)
+        wo_quantise(1, 1)
+        regroup(0, 1, nc.vector.tensor_copy)
+        quantise(0)
+        warm_up(2)
+        transposes(1)
+        regroup(1, 0)
+        regroup(1, 1)
+        add_bias(0, nc.vector)
+        matmuls(0)
         cols_ps = ps_zt.tile([P, D], F32, name="cols_ps", tag="zt")
         for b in range(2 * D // P):
             nc.tensor.matmul(
                 out=cols_ps[:, b:b + 1], lhsT=gb_rows[:, b * P:(b + 1) * P], rhs=ones[:, 0:1], start=True, stop=True
             )
         gb_cols = const.tile([P, 2 * D // P], F32)
-        wo_regroup(0, 0, nc.vector.tensor_copy)
-        wo_regroup(0, 1, nc.scalar.copy)
-        wo_regroup(1, 0, nc.vector.tensor_copy)
-        wo_regroup(1, 1, nc.scalar.copy)
-        for e in range(E):
-            for h in range(2):
-                wo_quantise(h, e)
-        transposes(1)
         gb_sb = const.tile([P, 2 * D], BF16)
-        regroup(1, 0)
-        regroup(1, 1)
-        add_bias(0, nc.vector)
-        matmuls(0)
         quantise(1)
         add_bias(1, nc.gpsimd)
         transposes(2)
@@ -373,10 +373,10 @@ def tile_heterogeneousgraphtransformer_pb_t_kernel(tc, att, scene_reps, Wo, bo, 
         regroup(3, 0)
         regroup(3, 1)
         inv_std(0)
-        centre_gain(0, 0)
-        centre_gain(0, 1)
         nc.vector.tensor_copy(out=gb_cols[:], in_=cols_ps[:, 0:2 * D // P])
         nc.vector.tensor_copy(out=gb_sb[:], in_=gb_ps[:])
+        centre_gain(0, 0)
+        centre_gain(0, 1)
         quantise(2)
         transposes(4)
         matmuls(2)
@@ -415,11 +415,12 @@ def tile_heterogeneousgraphtransformer_pb_t_kernel(tc, att, scene_reps, Wo, bo, 
             if not turned(m) and not on_gpsimd(m):
                 scale_shift(m, 0)
             if m == PAIRS - 1:
-                store_tile(m - 1, 0)
                 store_tile(m, 0)
             scale_shift(m, 1)
             if m >= PAIRS - 2:
                 store_tile(m, 1)
+                if m == PAIRS - 1:
+                    store_tile(m - 1, 0)
             elif not turned(m):
                 store(m)
             if n < PAIRS:

@@ -17,7 +17,7 @@ E = 2
 TOKENS = 4096
 TILES = TOKENS // P
 PAIRS = TILES // 2
-LOAD_TILES = (2, 2) + (4,) * ((TILES - 4) // 4)
+LOAD_TILES = (2,) * 6 + (4,) * ((TILES - 12) // 4)
 WORDS = D // 2
 EPS = 1e-5
 RING = 5
@@ -94,11 +94,9 @@ def tile_heterogeneousgraphtransformer_pb_t_kernel(tc, att, scene_reps, Wo, bo, 
         for t in range(1, 4):
             nc.sync.dma_start(out=wo_sb[t][:], in_=wo_v[:, t, :])
         load_att(0)
-        load_scene(0)
-        load_att(1)
-        load_scene(1)
-        for c in range(2, len(LOAD_TILES)):
-            load_att(c)
+        for c in range(len(LOAD_TILES)):
+            if c + 1 < len(LOAD_TILES):
+                load_att(c + 1)
             load_scene(c)
 
         wgrp = const.tile([P, E * D * 4], BF16, align_bytes=64)

@@ -209,10 +209,7 @@ def tile_heterogeneousgraphtransformer_pb_t_kernel(tc, att, scene_reps, Wo, bo, 
                 [P, 2 * D], F32, name="sb%d" % k, tag="ring%d" % (k % RING), align_bytes=64)
             att_tile, scene_tile, n, j0 = pair_load[k]
             engine.tensor_tensor(
-                out=sb_t[k][:].rearrange("p (j d) -> p j d", j=2),
-                in0=scene_tile[:, j0 * D:(j0 + 2) * D].rearrange("p (j d) -> p j d", j=2),
-                in1=bo_b[:].unsqueeze(1).to_broadcast([P, 2, D]),
-                op=ALU.add,
+                out=sb_t[k][:], in0=scene_tile[:, j0 * D:(j0 + 2) * D], in1=bo_b[:], op=ALU.add
             )
 
         def residual(k, i):
@@ -321,8 +318,9 @@ def tile_heterogeneousgraphtransformer_pb_t_kernel(tc, att, scene_reps, Wo, bo, 
         warm_up(4)
         bo_ps = ps_zt.tile([P, D], F32, name="bo_ps", tag="zt")
         nc.tensor.matmul(out=bo_ps[:], lhsT=ones[:, 0:P], rhs=bo_row[:], start=True, stop=True)
-        bo_b = const.tile([P, D], BF16)
-        nc.scalar.copy(out=bo_b[:], in_=bo_ps[:])
+        bo_b = const.tile([P, 2 * D], BF16)
+        for i in range(2):
+            nc.scalar.copy(out=bo_b[:, i * D:(i + 1) * D], in_=bo_ps[:])
         wo_transposes(0)
         wo_regroup(0, 0, nc.vector.tensor_copy)
         wo_regroup(0, 1, nc.scalar.copy)

@@ -37,7 +37,7 @@ def tile_heterogeneousgraphtransformer_pb_t_kernel(tc, att, scene_reps, Wo, bo, 
         ring_pool = ctx.enter_context(tc.tile_pool(name="ring", bufs=1))
         code_pool = ctx.enter_context(tc.tile_pool(name="code", bufs=3))
         zw_pool = ctx.enter_context(tc.tile_pool(name="zw", bufs=2))
-        o_pool = ctx.enter_context(tc.tile_pool(name="o", bufs=10))
+        o_pool = ctx.enter_context(tc.tile_pool(name="o", bufs=PAIRS))
         small = ctx.enter_context(tc.tile_pool(name="small", bufs=4))
         ps_const = ctx.enter_context(tc.psum_pool(name="psc", bufs=1))
         ps_zt = ctx.enter_context(tc.psum_pool(name="psz", bufs=1))

from contextlib import ExitStack

import concourse.mybir as mybir
from concourse.masks import make_identity

F32 = mybir.dt.float32
BF16 = mybir.dt.bfloat16
U32 = mybir.dt.uint32
U8 = mybir.dt.uint8
FP8X4 = mybir.dt.float8_e4m3fn_x4
ALU = mybir.AluOpType
ACT = mybir.ActivationFunctionType

P = 128
D = 512
E = 2
TOKENS = 4096
TILES = TOKENS // P
PAIRS = TILES // 2
LOAD_TILES = (2,) * 6 + (4,) * ((TILES - 12) // 4)
WORDS = D // 2
EPS = 1e-5
RING = 5
FLOPS = 2 * TOKENS * E * D * D


def tile_heterogeneousgraphtransformer_pb_t_kernel(tc, att, scene_reps, Wo, bo, gamma, beta, out):
    nc = tc.nc
    att_v = att.rearrange("e b s d -> e (b s) d").rearrange("e (p j) d -> p e j d", j=TILES)
    scene_v = scene_reps.rearrange("b s d -> (b s) d").rearrange("(p j) d -> p j d", j=TILES)
    out_v = out.rearrange("b s d -> (b s) d").rearrange("(p j) d -> p j d", j=TILES)
    wo_v = Wo.rearrange("(t p) k -> p t k", p=P)

    with ExitStack() as ctx:
        const = ctx.enter_context(tc.tile_pool(name="const", bufs=1))
        loads = ctx.enter_context(tc.tile_pool(name="loads", bufs=1))
        ring_pool = ctx.enter_context(tc.tile_pool(name="ring", bufs=1))
        code_pool = ctx.enter_context(tc.tile_pool(name="code", bufs=3))
        zw_pool = ctx.enter_context(tc.tile_pool(name="zw", bufs=2))
        o_pool = ctx.enter_context(tc.tile_pool(name="o", bufs=PAIRS))
        small = ctx.enter_context(tc.tile_pool(name="small", bufs=4))
        ps_const = ctx.enter_context(tc.psum_pool(name="psc", bufs=1))
        ps_zt = ctx.enter_context(tc.psum_pool(name="psz", bufs=1))
        ps_xt = ctx.enter_context(tc.psum_pool(name="psx", bufs=2))
        ps_f = ctx.enter_context(tc.psum_pool(name="psf", bufs=4))
        ctx.enter_context(tc.manual_schedule())

        ident = const.tile([P, P], F32)
        make_identity(nc, ident[:])
        bo_row = const.tile([P, D], BF16)
        nc.vector.memset(bo_row[:].bitcast(U32), 0)
        ones = const.tile([P, D], BF16)
        nc.vector.memset(ones[:], 1.0)

        def warm_up(n):
            scratch = ps_zt.tile([P, D], F32, name="scratch%d" % n, tag="zt")
            for i in range(n):
                nc.tensor.matmul(out=scratch[:], lhsT=ones[:, 0:P], rhs=ones[:], start=True, stop=True)

        gb_rows = const.tile([P, 2 * D], BF16)
        nc.vector.memset(gb_rows[:].bitcast(U32), 0)
        eps_t = const.tile([P, 1], F32)
        nc.vector.memset(eps_t[:], EPS)
        squares_out = const.tile([P, 2 * D], F32)

        warm = const.tile([P, 1], F32)
        nc.scalar.activation(out=warm[:], in_=eps_t[:], func=ACT.Abs_reciprocal_sqrt)

        pair_load = []
        att_t = []
        scene_t = []
        for c, n in enumerate(LOAD_TILES):
            att_t.append(loads.tile([P, E * n * D], BF16, name="att%d" % c))
            scene_t.append(loads.tile([P, n * D], BF16, name="scene%d" % c))
            for j in range(0, n, 2):
                pair_load.append((att_t[c], scene_t[c], n, j))

        def load_att(c):
            g, n = sum(LOAD_TILES[:c]), LOAD_TILES[c]
            nc.sync.dma_start(out=att_t[c][:].rearrange("p (e j d) -> p e j d", e=E, j=n), in_=att_v[:, :, g:g + n, :])

        def load_scene(c):
            g, n = sum(LOAD_TILES[:c]), LOAD_TILES[c]
            nc.sync.dma_start(out=scene_t[c][:].rearrange("p (j d) -> p j d", j=n), in_=scene_v[:, g:g + n, :])

        wo_sb = []
        for t in range(4):
            wo_sb.append(const.tile([P, E * D], BF16, name="wo%d" % t))
        for t in range(0, 1):
            nc.sync.dma_start(out=wo_sb[t][:], in_=wo_v[:, t, :])
        nc.sync.dma_start(out=bo_row[0:1, :], in_=bo.rearrange("(o d) -> o d", o=1))
        for i, v in enumerate((gamma, beta)):
            nc.sync.dma_start(out=gb_rows[0:1, i * D:(i + 1) * D], in_=v.rearrange("(o d) -> o d", o=1))
        for t in range(1, 4):
            nc.sync.dma_start(out=wo_sb[t][:], in_=wo_v[:, t, :])
        load_att(0)
        for c in range(len(LOAD_TILES)):
            if c + 1 < len(LOAD_TILES):
                load_att(c + 1)
            load_scene(c)

        wgrp = const.tile([P, E * D * 4], BF16, align_bytes=64)
        wgrp_f = wgrp[:].bitcast(F32)
        wcodes = const.tile([P, E * D], U32, align_bytes=64)
        wscl = const.tile([P, E * D], U8, align_bytes=64)
        wt_t = {}

        def wo_transposes(h):
            for e in range(E):
                wt_t[(h, e)] = ps_f.tile([P, D], F32, name="wt%d%d" % (h, e), tag="f")
            for t in range(2):
                wo_f = wo_sb[2 * h + t][:].bitcast(F32)
                for e in range(E):
                    for u in range(2):
                        nc.tensor.transpose(
                            out=wt_t[(h, e)][:, (t * 2 + u) * P:(t * 2 + u + 1) * P],
                            in_=wo_f[:, e * WORDS + u:(e + 1) * WORDS:2], identity=ident[:],
                        )

        def wo_regroup(h, e, copy):
            copy(
                out=wgrp_f[:, (e * D + h * 2 * P) * 2:(e * D + (h + 1) * 2 * P) * 2].rearrange(
                    "p (t r u) -> p t r u", t=2, u=2),
                in_=wt_t[(h, e)][:].rearrange("p (t u r) -> p t r u", t=2, u=2),
            )

        def wo_quantise(h, e):
            c0 = e * D + h * 2 * P
            nc.vector.quantize_mx(
                out=wcodes[:, c0:c0 + 2 * P].bitcast(FP8X4),
                scales=wscl[:, c0:c0 + 2 * P],
                in_=wgrp[:, 4 * c0:4 * (c0 + 2 * P)],
            )

        xt_t = {}
        grp_t = {}
        code_t = {}
        scl_t = {}
        sb_t = {}
        f_t = {}
        o_t = {}
        sums_t = {}
        negmean_t = {}
        sumsq_t = {}
        rstd_t = {}
        shift_t = {}
        z_t = {}
        zt_t = {}
        w_t = {}
        bk_t = {}

        def transposes(k):
            if k >= PAIRS:
                return
            att_tile, scene_tile, n, j0 = pair_load[k]
            a_f = att_tile[:].bitcast(F32)
            for i in range(2):
                j = j0 + i
                xt = ps_xt.tile([P, D], F32, name="xt%d_%d" % (k, i), tag="xt")
                xt_t[(k, i)] = xt
                for e in range(E):
                    for u in range(2):
                        w0 = (e * n + j) * WORDS
                        nc.tensor.transpose(
                            out=xt[:, (e * 2 + u) * P:(e * 2 + u + 1) * P], in_=a_f[:, w0 + u:w0 + WORDS:2],
                            identity=ident[:],
                        )

        def regroup(k, i, copy=nc.scalar.copy):
            if k >= PAIRS:
                return
            if i == 0:
                grp_t[k] = ring_pool.tile([P, 2 * E * P * 4], BF16, name="grp%d" % k, tag="ring%d" % (k % RING), align_bytes=64)
            g_f = grp_t[k][:].bitcast(F32)
            copy(
                out=g_f[:, i * D:(i + 1) * D].rearrange("p (e r u) -> p e r u", e=E, u=2),
                in_=xt_t[(k, i)][:].rearrange("p (e u r) -> p e r u", e=E, u=2),
            )

        def quantise(k):
            if k >= PAIRS:
                return
            code_t[k] = code_pool.tile([P, 2 * E * P], U32, name="cd%d" % k, tag="cd", align_bytes=64)
            scl_t[k] = code_pool.tile([P, 2 * E * P], U8, name="sc%d" % k, tag="sc", align_bytes=64)
            nc.vector.quantize_mx(out=code_t[k][:].bitcast(FP8X4), scales=scl_t[k][:], in_=grp_t[k][:])

        def matmuls(k):
            if k >= PAIRS:
                return
            for i in range(2):
                f = ps_f.tile([P, D], F32, name="f%d_%d" % (k, i), tag="f")
                f_t[(k, i)] = f
                for e in range(E):
                    cols = slice((i * E + e) * P, (i * E + e + 1) * P)
                    nc.tensor.matmul_mx(
                        out=f[:],
                        lhsT=code_t[k][:, cols].bitcast(FP8X4),
                        lhsT_scale=scl_t[k][:, cols],
                        rhs=wcodes[:, e * D:(e + 1) * D].bitcast(FP8X4),
                        rhs_scale=wscl[:, e * D:(e + 1) * D],
                        start=(e == 0),
                        stop=(e == E - 1),
                    )

        def add_bias(k, engine):
            if k >= PAIRS:
                return
            sb_t[k] = ring_pool.tile(
                [P, 2 * D], F32, name="sb%d" % k, tag="ring%d" % (k % RING), align_bytes=64)
            att_tile, scene_tile, n, j0 = pair_load[k]
            engine.tensor_tensor(
                out=sb_t[k][:], in0=scene_tile[:, j0 * D:(j0 + 2) * D], in1=bo_b[:], op=ALU.add
            )

        def residual(k, i):
            if i == 0:
                sums_t[k] = small.tile([P, 2], F32, name="sums%d" % k, tag="sums")
            y = sb_t[k][:, i * D:(i + 1) * D]
            nc.vector.scalar_tensor_tensor(
                out=y, in0=y, scalar=1.0, in1=f_t[(k, i)][:], op0=ALU.mult, op1=ALU.add,
                accum_out=sums_t[k][:, i:i + 1],
            )

        def neg_mean(k):
            negmean_t[k] = small.tile([P, 2], F32, name="negmean%d" % k, tag="negmean")
            nc.scalar.activation(out=negmean_t[k][:], in_=sums_t[k][:], func=ACT.Copy, scale=-1.0 / D)

        def squares(k, i):
            if i == 0:
                sumsq_t[k] = small.tile([P, 2], F32, name="sumsq%d" % k, tag="sumsq")
            nc.scalar.activation(
                out=squares_out[:, i * D:(i + 1) * D], in_=sb_t[k][:, i * D:(i + 1) * D], func=ACT.Square,
                bias=negmean_t[k][:, i:i + 1], scale=1.0, accum_out=sumsq_t[k][:, i:i + 1],
            )

        def inv_std(k, i=0, n=2):
            if k not in rstd_t:
                rstd_t[k] = small.tile([P, 2], F32, name="rstd%d" % k, tag="rstd")
            nc.scalar.activation(
                out=rstd_t[k][:, i:i + n], in_=sumsq_t[k][:, i:i + n], func=ACT.Abs_reciprocal_sqrt, bias=eps_t[:],
                scale=1.0 / D,
            )

        def out_tile(k):
            if k not in o_t:
                o_t[k] = o_pool.tile([P, 2 * D], F32, name="o%d" % k, tag="o")
            return o_t[k]

        def centre_gain(k, i):
            nc.vector.scalar_tensor_tensor(
                out=out_tile(k)[:, i * D:(i + 1) * D], in0=sb_t[k][:, i * D:(i + 1) * D],
                scalar=negmean_t[k][:, i:i + 1], in1=gb_ps[:, 0:D], op0=ALU.add, op1=ALU.mult,
            )

        def scale_shift(k, i):
            o = o_t[k][:, i * D:(i + 1) * D]
            nc.vector.scalar_tensor_tensor(
                out=o, in0=o, scalar=rstd_t[k][:, i:i + 1], in1=gb_ps[:, D:2 * D], op0=ALU.mult, op1=ALU.add
            )

        def late(k):
            return k >= PAIRS - 3

        def on_gpsimd(k):
            return late(k) and k < PAIRS - 1

        def neg_mean_rstd(k):
            shift_t[k] = small.tile([P, 1], F32, name="shift%d" % k, tag="shift")
            nc.scalar.activation(
                out=shift_t[k][:], in_=negmean_t[k][:, 0:1], func=ACT.Copy, scale=rstd_t[k][:, 0:1]
            )

        def standardise(k):
            z_t[k] = zw_pool.tile([P, D], F32, name="z%d" % k, tag="z")
            nc.scalar.activation(
                out=z_t[k][:], in_=sb_t[k][:, 0:D], func=ACT.Identity, scale=rstd_t[k][:, 0:1], bias=shift_t[k][:]
            )

        def gain_shift_gpsimd(k):
            o = out_tile(k)[:, 0:D]
            w = zw_pool.tile([P, D], F32, name="w%d" % k, tag="w")
            nc.gpsimd.tensor_tensor(out=w[:], in0=z_t[k][:], in1=gb_sb[:, 0:D], op=ALU.mult)
            nc.gpsimd.tensor_tensor(out=o, in0=w[:], in1=gb_sb[:, D:2 * D], op=ALU.add)

        def turned(k):
            return 0 < k < PAIRS - 4 and k % 2 == 1

        def turn(k):
            zt_t[k] = ps_zt.tile([P, D], F32, name="zt%d" % k, tag="zt")
            for b in range(D // P):
                cols = slice(b * P, (b + 1) * P)
                nc.tensor.transpose(out=zt_t[k][:, cols], in_=z_t[k][:, cols], identity=ident[:])

        def gain_shift(k):
            w_t[k] = zw_pool.tile([P, D], F32, name="w%d" % k, tag="w")
            for b in range(D // P):
                cols = slice(b * P, (b + 1) * P)
                nc.scalar.activation(
                    out=w_t[k][:, cols], in_=zt_t[k][:, cols], func=ACT.Identity,
                    scale=gb_cols[:, b:b + 1], bias=gb_cols[:, D // P + b:D // P + b + 1],
                )

        def turn_back(k):
            bk_t[k] = ps_zt.tile([P, D], F32, name="bk%d" % k, tag="zt")
            for b in range(D // P):
                cols = slice(b * P, (b + 1) * P)
                nc.tensor.transpose(out=bk_t[k][:, cols], in_=w_t[k][:, cols], identity=ident[:])

        def copy_out(k):
            nc.scalar.copy(out=out_tile(k)[:, 0:D], in_=bk_t[k][:])

        def store_tile(k, i):
            nc.sync.dma_start(out=out_v[:, 2 * k + i, :], in_=o_t[k][:, i * D:(i + 1) * D])

        def store(k):
            nc.sync.dma_start(out=out_v[:, 2 * k:2 * k + 2, :], in_=o_t[k][:].rearrange("p (j d) -> p j d", j=2))

        warm_up(4)
        bo_ps = ps_zt.tile([P, D], F32, name="bo_ps", tag="zt")
        nc.tensor.matmul(out=bo_ps[:], lhsT=ones[:, 0:P], rhs=bo_row[:], start=True, stop=True)
        bo_b = const.tile([P, 2 * D], BF16)
        for i in range(2):
            nc.scalar.copy(out=bo_b[:, i * D:(i + 1) * D], in_=bo_ps[:])
        wo_transposes(0)
        wo_regroup(0, 0, nc.vector.tensor_copy)
        wo_regroup(0, 1, nc.scalar.copy)
        gb_ps = ps_const.tile([P, 2 * D], BF16)
        for v in range(2):
            nc.tensor.matmul(
                out=gb_ps[:, v * D:(v + 1) * D], lhsT=ones[:, 0:P], rhs=gb_rows[:, v * D:(v + 1) * D], start=True, stop=True
            )
        wo_transposes(1)
        wo_quantise(0, 0)
        wo_regroup(1, 0, nc.vector.tensor_copy)
        wo_regroup(1, 1, nc.scalar.copy)
        transposes(0)
        regroup(0, 0, nc.scalar.copy)
        wo_quantise(0, 1)
        wo_quantise(1, 0)
        wo_quantise(1, 1)
        regroup(0, 1, nc.vector.tensor_copy)
        quantise(0)
        warm_up(2)
        transposes(1)
        regroup(1, 0)
        regroup(1, 1)
        add_bias(0, nc.vector)
        matmuls(0)
        cols_ps = ps_zt.tile([P, D], F32, name="cols_ps", tag="zt")
        for b in range(2 * D // P):
            nc.tensor.matmul(
                out=cols_ps[:, b:b + 1], lhsT=gb_rows[:, b * P:(b + 1) * P], rhs=ones[:, 0:1], start=True, stop=True
            )
        gb_cols = const.tile([P, 2 * D // P], F32)
        gb_sb = const.tile([P, 2 * D], BF16)
        quantise(1)
        add_bias(1, nc.gpsimd)
        transposes(2)
        matmuls(1)

        residual(0, 0)
        residual(0, 1)
        regroup(2, 0)
        neg_mean(0)
        regroup(2, 1)
        transposes(3)
        squares(0, 0)
        squares(0, 1)
        regroup(3, 0)
        regroup(3, 1)
        inv_std(0)
        nc.vector.tensor_copy(out=gb_cols[:], in_=cols_ps[:, 0:2 * D // P])
        nc.vector.tensor_copy(out=gb_sb[:], in_=gb_ps[:])
        centre_gain(0, 0)
        centre_gain(0, 1)
        quantise(2)
        transposes(4)
        matmuls(2)
        add_bias(2, nc.gpsimd)

        for n in range(1, PAIRS + 1):
            m = n - 1
            if n < PAIRS:
                residual(n, 0)
                residual(n, 1)
                regroup(n + 3, 0)
                if turned(m):
                    neg_mean_rstd(m)
                neg_mean(n)
                if turned(m):
                    standardise(m)
                regroup(n + 3, 1)
                transposes(n + 4)
                if turned(m):
                    turn(m)
                squares(n, 0)
                if late(n):
                    inv_std(n, 0, 1)
                squares(n, 1)
                if on_gpsimd(n):
                    neg_mean_rstd(n)
                if late(n):
                    inv_std(n, 1, 1)
                if on_gpsimd(n):
                    standardise(n)
            if turned(n - 2):
                copy_out(n - 2)
                store(n - 2)
            if not late(n):
                inv_std(n)
            if not turned(m) and not on_gpsimd(m):
                scale_shift(m, 0)
            if m == PAIRS - 1:
                store_tile(m, 0)
            scale_shift(m, 1)
            if m >= PAIRS - 2:
                store_tile(m, 1)
                if m == PAIRS - 1:
                    store_tile(m - 1, 0)
            elif not turned(m):
                store(m)
            if n < PAIRS:
                if not turned(n) and not on_gpsimd(n):
                    centre_gain(n, 0)
                if turned(m):
                    gain_shift(m)
                quantise(n + 2)
                add_bias(n + 2, nc.gpsimd)
                matmuls(n + 2)
                if on_gpsimd(n):
                    gain_shift_gpsimd(n)
                if turned(m):
                    turn_back(m)
                centre_gain(n, 1)
